import numpy as np
import ml_dtypes


def mxq(x, axis, fmt="e4m3"):
    dtype, down = {"e4m3": (ml_dtypes.float8_e4m3fn, 7), "e5m2": (ml_dtypes.float8_e5m2, 14)}[fmt]
    v = np.moveaxis(np.asarray(x, np.float32).astype(ml_dtypes.bfloat16).astype(np.float64), axis, -1)
    blocks = v.reshape(v.shape[:-1] + (-1, 32))
    amax = np.abs(blocks).max(-1, keepdims=True)
    byte = np.maximum(np.where(amax > 0, np.frexp(amax)[1] - 1 + 127, 0) - down, 1)
    scale = np.exp2(byte - 127.0)
    codes = (blocks / scale).astype(np.float32).astype(dtype).astype(np.float64)
    return np.moveaxis((codes * scale).reshape(v.shape), -1, axis)


WIDE = False


def mx_kscale(k):
    if not WIDE:
        return np.ones(k)
    levels = np.array([10, -10, 5, -5, 0])
    a = np.random.permutation(np.resize(levels, k // 512 * 4)).reshape(k // 512, 4)
    idx = np.arange(k)
    return np.exp2(a[idx // 512, idx % 128 // 32])


BF16 = ml_dtypes.bfloat16


def bf(x):
    return np.asarray(x, np.float32).astype(BF16)


def f64(x):
    return np.asarray(x).astype(np.float64)


E2M1 = np.array([0.0, 0.5, 1.0, 1.5, 2.0, 3.0, 4.0, 6.0, -0.0, -0.5, -1.0, -1.5, -2.0, -3.0, -4.0, -6.0])


def pack_weight(w, fmt):
    k, n = w.shape
    w = f64(bf(w)).reshape(k // 32, 32, n)
    amax = np.abs(w).max(1)
    if fmt == "e4m3":
        byte = np.frexp(amax)[1] - 1 + 127 - 7
    else:
        mant, ex = np.frexp(amax / 6.0)
        byte = np.where(mant > 0.5, ex, ex - 1) + 127
    byte = np.clip(np.where(amax > 0, byte, 1), 1, 254)
    scaled = (w * np.exp2(127.0 - byte)[:, None, :]).reshape(k, n).astype(np.float32)
    by_word = np.ascontiguousarray(scaled.reshape(k // 512, 128, 4, n).transpose(0, 1, 3, 2))
    if fmt == "e4m3":
        words = by_word.astype(ml_dtypes.float8_e4m3fn).view(np.uint8)
    else:
        c = by_word.astype(ml_dtypes.float4_e2m1fn).view(np.uint8) & 0xF
        words = c[..., 0::2] | (c[..., 1::2] << 4)
    return np.ascontiguousarray(words), np.ascontiguousarray(byte.astype(np.uint8).reshape(k // 512, 16, n))


def unpack_weight(words, scales, fmt):
    g, p, n, _ = words.shape
    if fmt == "e4m3":
        vals = np.ascontiguousarray(words).view(ml_dtypes.float8_e4m3fn).astype(np.float64)
    else:
        nib = np.empty((g, p, n, 4), np.uint8)
        nib[..., 0::2] = words & 0xF
        nib[..., 1::2] = words >> 4
        vals = E2M1[nib]
    vals = vals * np.repeat(np.exp2(scales.astype(np.float64) - 127.0), 8, axis=1)[..., None]
    return vals.transpose(0, 1, 3, 2).reshape(g * 512, n)

def pack4(w):
    words, scales = pack_weight(w, "e2m1")
    return words.reshape(words.shape[0], 128, -1), scales


def unpack4(words, scales):
    return unpack_weight(words.reshape(words.shape[0], 128, -1, 2), scales, "e2m1")


B, S, D, DM, DK = 2, 256, 512, 16384, 64
LN_EPS = 1e-5


def setup_inputs():
    s = mx_kscale(DM)
    h_attn = bf(np.random.standard_normal((B, S, DM)) * 0.3 * s)
    Wo_words, Wo_scales = pack4(np.random.standard_normal((DM, D)) * 3.0 / np.sqrt(DM) / s[:, None])
    return {
        "h_attn": h_attn,
        "Wo_words": Wo_words,
        "Wo_scales": Wo_scales,
        "bo": bf(np.random.standard_normal((B, S, D)) * 0.5 + np.random.uniform(0.25, 0.75, (B, 1, 1))),
        "x": bf(np.random.standard_normal((B, S, D))),
        "gamma": bf(1.0 + 0.1 * np.random.standard_normal((S, D))),
        "beta": bf(0.1 * np.random.standard_normal((S, D))),
    }


def reference(h_attn, Wo_words, Wo_scales, bo, x, gamma, beta):
    o = (mxq(f64(h_attn), 2, "e4m3") @ unpack4(Wo_words, Wo_scales)) + f64(bo)
    o = o + f64(x)
    mu = o.mean(axis=(-2, -1), keepdims=True)
    var = np.square(o - mu).mean(axis=(-2, -1), keepdims=True)
    return (o - mu) / np.sqrt(var + LN_EPS) * f64(gamma) + f64(beta)

@@ -1,0 +1,257 @@
+from contextlib import ExitStack
+
+import concourse.masks as masks
+import concourse.mybir as mybir
+
+F32 = mybir.dt.float32
+BF16 = mybir.dt.bfloat16
+I32 = mybir.dt.int32
+U32 = mybir.dt.uint32
+U8 = mybir.dt.uint8
+FP8X4 = mybir.dt.float8_e4m3fn_x4
+FP4X4 = mybir.dt.float4_e2m1fn_x4
+ALU = mybir.AluOpType
+ACT = mybir.ActivationFunctionType
+AXIS = mybir.AxisListType
+
+BATCH, SEQ, D, K = 2, 256, 512, 16384
+LN_EPS = 1e-5
+
+P = 128
+PACK = 4
+K_PASS = P * PACK
+HALVES = 2
+TILES = SEQ // P
+CHUNK = 4
+CHUNKS = K // (K_PASS * CHUNK)
+K_CHUNK = K_PASS * CHUNK
+BANK_PASSES = 2
+PREFETCH = 4
+
+FLOPS = 2 * BATCH * SEQ * K * D
+
+
+def tile_multiheadattn_pb_k_kernel(tc, h_attn, Wo_words, Wo_scales, bo, x, gamma, beta, out):
+    nc = tc.nc
+
+    rounds = [(c, b) for c in range(CHUNKS - 2) for b in range(BATCH)]
+    first_late_round = len(rounds)
+    rounds += [(c, b) for b in range(BATCH) for c in range(CHUNKS - 2, CHUNKS)]
+    n_rounds = len(rounds)
+    last_round = [rounds.index((CHUNKS - 1, b)) for b in range(BATCH)]
+
+    with ExitStack() as ctx:
+        consts = ctx.enter_context(tc.tile_pool(name="consts", bufs=1))
+        weights = ctx.enter_context(tc.tile_pool(name="weights", bufs=1))
+        raw_pool = ctx.enter_context(tc.tile_pool(name="raw", bufs=TILES * PREFETCH))
+        stage = ctx.enter_context(tc.tile_pool(name="stage", bufs=2))
+        norm = ctx.enter_context(tc.tile_pool(name="norm", bufs=1))
+        psum_acc = ctx.enter_context(tc.psum_pool(name="psum_acc", bufs=1))
+        psum_work = ctx.enter_context(tc.psum_pool(name="psum_work", bufs=4))
+        ctx.enter_context(tc.manual_schedule())
+
+        identity = consts.tile([P, P], F32)
+        masks.make_identity(nc, identity[:])
+        averager = consts.tile([P, P], F32)
+        nc.vector.memset(averager[:], 1.0 / (SEQ * D))
+        eps = consts.tile([P, 1], F32)
+        nc.vector.memset(eps[:], LN_EPS)
+        warm = consts.tile([P, 1], F32)
+        nc.scalar.activation(out=warm[:], in_=eps[:], func=ACT.Sqrt)
+
+        w_words = []
+        w_scales = []
+        for c in range(CHUNKS):
+            words = weights.tile([P, CHUNK * 2 * D], U8, name="w_words%d" % c, align_bytes=64)
+            plane = weights.tile([P, CHUNK * D], U8, name="w_scales%d" % c, align_bytes=64)
+            nc.vector.memset(plane[:].bitcast(I32), 0)
+            w_words.append(words)
+            w_scales.append(plane)
+        dram_words = Wo_words.bitcast(I32)
+        dram_scales = Wo_scales.bitcast(I32)
+
+        acc = [
+            [psum_acc.tile([P, D], F32, name="acc%d%d" % (b, t)) for t in range(TILES)]
+            for b in range(BATCH)
+        ]
+
+        bo_sb = norm.tile([P, BATCH, TILES * D], BF16)
+        x_sb = norm.tile([P, BATCH, TILES * D], BF16)
+        gamma_sb = norm.tile([P, TILES * D], BF16)
+        beta_sb = norm.tile([P, TILES * D], BF16)
+
+        raw_tiles = {}
+        ordered_tiles = {}
+        grouped_tiles = {}
+        code_tiles = {}
+        fetched_chunks = set()
+        batch_tiles = [{} for b in range(BATCH)]
+
+        def fetch_weights(c):
+            passes = slice(c * CHUNK, (c + 1) * CHUNK)
+            for r in range(4):
+                nc.sync.dma_start(
+                    out=w_scales[c][r:P:32, :].bitcast(I32).rearrange("q (g n) -> q g n", g=CHUNK),
+                    in_=dram_scales[passes, r:16:4, :].rearrange("g q n -> q g n"),
+                )
+            nc.sync.dma_start(
+                out=w_words[c][:].bitcast(I32).rearrange("p (g n) -> p g n", g=CHUNK),
+                in_=dram_words[passes].rearrange("g p n -> p g n"),
+            )
+
+        def fetch(r):
+            if r == first_late_round:
+                nc.sync.dma_start(out=bo_sb[:], in_=bo.rearrange("b (p t) d -> p b (t d)", t=TILES))
+                nc.sync.dma_start(out=x_sb[:], in_=x.rearrange("b (p t) d -> p b (t d)", t=TILES))
+            if r < n_rounds:
+                c, b = rounds[r]
+                by_tile = h_attn[b].rearrange("(p t) k -> t p k", t=TILES)
+                for t in range(TILES):
+                    raw = raw_pool.tile([P, K_CHUNK], BF16)
+                    nc.sync.dma_start(out=raw[:], in_=by_tile[t, :, c * K_CHUNK : (c + 1) * K_CHUNK])
+                    raw_tiles[(r, t)] = raw
+            if 1 <= r <= n_rounds and rounds[r - 1][0] not in fetched_chunks:
+                fetched_chunks.add(rounds[r - 1][0])
+                fetch_weights(rounds[r - 1][0])
+            if r == n_rounds - 1:
+                nc.sync.dma_start(out=gamma_sb[:], in_=gamma.rearrange("(p t) d -> p (t d)", t=TILES))
+                nc.sync.dma_start(out=beta_sb[:], in_=beta.rearrange("(p t) d -> p (t d)", t=TILES))
+
+        def sort_words(r):
+            ordered = stage.tile([P, TILES, CHUNK, HALVES, P], F32)
+            for t in range(TILES):
+                nc.vector.tensor_copy(
+                    out=ordered[:, t],
+                    in_=raw_tiles[(r, t)][:].bitcast(F32).rearrange("r (g p u) -> r g u p", g=CHUNK, u=HALVES),
+                )
+            ordered_tiles[r] = ordered
+
+        def transpose(r):
+            ordered = ordered_tiles[r]
+            grouped = stage.tile([P, TILES * CHUNK * P * PACK], BF16, align_bytes=64)
+            grouped_words = grouped[:].bitcast(F32).rearrange(
+                "p (t g r u) -> p t g r u", t=TILES, g=CHUNK, u=HALVES
+            )
+            for t in range(TILES):
+                for g0 in range(0, CHUNK, BANK_PASSES):
+                    flipped = psum_work.tile([P, BANK_PASSES, HALVES, P], F32, tag="work")
+                    for g in range(BANK_PASSES):
+                        for u in range(HALVES):
+                            nc.tensor.transpose(flipped[:, g, u, :], ordered[:, t, g0 + g, u, :], identity[:])
+                    nc.scalar.copy(
+                        out=grouped_words[:, t, g0 : g0 + BANK_PASSES],
+                        in_=flipped[:].rearrange("p g u r -> p g r u"),
+                    )
+            grouped_tiles[r] = grouped
+
+        def quantise(r):
+            grouped = grouped_tiles[r]
+            codes = stage.tile([P, TILES * CHUNK * P], U32, align_bytes=64)
+            h_scales = stage.tile([P, TILES * CHUNK * P], U8, align_bytes=64)
+            per_tile = CHUNK * P
+            for t in range(TILES):
+                cols = slice(t * per_tile, (t + 1) * per_tile)
+                nc.vector.quantize_mx(
+                    out=codes[:, cols].bitcast(FP8X4),
+                    scales=h_scales[:, cols],
+                    in_=grouped[:, t * per_tile * PACK : (t + 1) * per_tile * PACK],
+                )
+            code_tiles[r] = (codes, h_scales)
+
+        def multiply(r):
+            c, b = rounds[r]
+            codes, h_scales = code_tiles[r]
+            for t in range(TILES):
+                for g in range(CHUNK):
+                    tokens = slice((t * CHUNK + g) * P, (t * CHUNK + g + 1) * P)
+                    nc.tensor.matmul_mx(
+                        out=acc[b][t][:],
+                        lhsT=codes[:, tokens].bitcast(FP8X4),
+                        lhsT_scale=h_scales[:, tokens],
+                        rhs=w_words[c][:, g * 2 * D : (g + 1) * 2 * D].bitcast(FP4X4),
+                        rhs_scale=w_scales[c][:, g * D : (g + 1) * D],
+                        start=(c == 0 and g == 0),
+                        stop=(c == CHUNKS - 1 and g == CHUNK - 1),
+                    )
+
+        def add_bias_to_residual(b):
+            extra = norm.tile([P, TILES * D], F32, name="extra%d" % b)
+            nc.vector.tensor_tensor(out=extra[:], in0=bo_sb[:, b, :], in1=x_sb[:, b, :], op=ALU.add)
+            batch_tiles[b]["extra"] = extra
+
+        def sum_and_mean(b):
+            o = norm.tile([P, TILES * D], F32, name="o%d" % b)
+            row_sums = norm.tile([P, TILES], F32, name="row_sums%d" % b)
+            for t in range(TILES):
+                cols = slice(t * D, (t + 1) * D)
+                nc.vector.scalar_tensor_tensor(
+                    out=o[:, cols],
+                    in0=acc[b][t][:],
+                    scalar=1.0,
+                    in1=batch_tiles[b]["extra"][:, cols],
+                    op0=ALU.mult,
+                    op1=ALU.add,
+                    accum_out=row_sums[:, t : t + 1],
+                )
+            mean_parts = psum_work.tile([P, TILES], F32, tag="work")
+            nc.tensor.matmul(out=mean_parts[:], lhsT=averager[:], rhs=row_sums[:], start=True, stop=True)
+            mean = norm.tile([P, 1], F32, name="mean%d" % b)
+            nc.vector.tensor_reduce(out=mean[:], in_=mean_parts[:], axis=AXIS.X, op=ALU.add)
+            batch_tiles[b]["o"] = o
+            batch_tiles[b]["mean"] = mean
+
+        def centre(b):
+            o = batch_tiles[b]["o"]
+            mean = batch_tiles[b]["mean"]
+            squares = norm.tile([P, TILES * D], F32, name="squares%d" % b)
+            square_sums = norm.tile([P, 1], F32, name="square_sums%d" % b)
+            nc.scalar.activation(
+                out=squares[:], in_=o[:], func=ACT.Square, bias=mean[:], scale=-1.0, accum_out=square_sums[:]
+            )
+            centred = norm.tile([P, TILES * D], F32, name="centred%d" % b)
+            nc.vector.scalar_tensor_tensor(
+                out=centred[:], in0=o[:], scalar=mean[:], in1=gamma_sb[:], op0=ALU.subtract, op1=ALU.mult
+            )
+            variance = psum_work.tile([P, 1], F32, tag="work")
+            nc.tensor.matmul(out=variance[:], lhsT=averager[:], rhs=square_sums[:], start=True, stop=True)
+            batch_tiles[b]["centred"] = centred
+            batch_tiles[b]["variance"] = variance
+
+        def normalise_and_store(b):
+            std = norm.tile([P, 1], F32, name="std%d" % b)
+            nc.scalar.activation(out=std[:], in_=batch_tiles[b]["variance"][:], func=ACT.Sqrt, bias=eps[:])
+            inv_std = norm.tile([P, 1], F32, name="inv_std%d" % b)
+            nc.vector.reciprocal(out=inv_std[:], in_=std[:])
+            result = norm.tile([P, TILES * D], F32, name="result%d" % b)
+            nc.vector.scalar_tensor_tensor(
+                out=result[:],
+                in0=batch_tiles[b]["centred"][:],
+                scalar=inv_std[:],
+                in1=beta_sb[:],
+                op0=ALU.mult,
+                op1=ALU.add,
+            )
+            nc.sync.dma_start(out=out[b].rearrange("(p t) d -> p (t d)", t=TILES), in_=result[:])
+
+        for r in range(PREFETCH):
+            fetch(r)
+        for i in range(n_rounds + 4):
+            if i < n_rounds:
+                sort_words(i)
+                fetch(i + PREFETCH)
+                if rounds[i][0] == CHUNKS - 2:
+                    add_bias_to_residual(rounds[i][1])
+            if 0 <= i - 1 < n_rounds:
+                transpose(i - 1)
+            if 0 <= i - 2 < n_rounds:
+                quantise(i - 2)
+            for b in range(BATCH):
+                if i == last_round[b] + 4:
+                    centre(b)
+                if i == last_round[b] + 3:
+                    sum_and_mean(b)
+            if 0 <= i - 2 < n_rounds:
+                multiply(i - 2)
+            for b in range(BATCH):
+                if i == last_round[b] + 4:
+                    normalise_and_store(b)

@@ -236,6 +236,8 @@ def tile_multiheadattn_pb_k_kernel(tc, h_attn, Wo_words, Wo_scales, bo, x, gamma
         for r in range(PREFETCH):
             fetch(r)
         for i in range(n_rounds + 4):
+            if 0 <= i - 2 < n_rounds:
+                quantise(i - 2)
             if i < n_rounds:
                 sort_words(i)
                 fetch(i + PREFETCH)
@@ -243,8 +245,6 @@ def tile_multiheadattn_pb_k_kernel(tc, h_attn, Wo_words, Wo_scales, bo, x, gamma
                     add_bias_to_residual(rounds[i][1])
             if 0 <= i - 1 < n_rounds:
                 transpose(i - 1)
-            if 0 <= i - 2 < n_rounds:
-                quantise(i - 2)
             for b in range(BATCH):
                 if i == last_round[b] + 4:
                     centre(b)

@@ -22,9 +22,15 @@ PACK = 4
 K_PASS = P * PACK
 HALVES = 2
 TILES = SEQ // P
-CHUNK = 4
-CHUNKS = K // (K_PASS * CHUNK)
-K_CHUNK = K_PASS * CHUNK
+CHUNK_PASSES = (4,) * 8
+CHUNKS = len(CHUNK_PASSES)
+FIRST_PASS = [sum(CHUNK_PASSES[:c]) for c in range(CHUNKS)]
+LATE = 2
+STORE_PIECES = 2
+QUAD = 4
+QUADS = K // (K_PASS * QUAD)
+MERGED_PASSES = 2
+assert sum(CHUNK_PASSES) * K_PASS == K
 BANK_PASSES = 2
 PREFETCH = 4
 
@@ -34,16 +40,16 @@ FLOPS = 2 * BATCH * SEQ * K * D
 def tile_multiheadattn_pb_k_kernel(tc, h_attn, Wo_words, Wo_scales, bo, x, gamma, beta, out):
     nc = tc.nc
 
-    rounds = [(c, b) for c in range(CHUNKS - 2) for b in range(BATCH)]
+    rounds = [(c, b) for c in range(CHUNKS - LATE) for b in range(BATCH)]
     first_late_round = len(rounds)
-    rounds += [(c, b) for b in range(BATCH) for c in range(CHUNKS - 2, CHUNKS)]
+    rounds += [(c, b) for b in range(BATCH) for c in range(CHUNKS - LATE, CHUNKS)]
     n_rounds = len(rounds)
     last_round = [rounds.index((CHUNKS - 1, b)) for b in range(BATCH)]
 
     with ExitStack() as ctx:
         consts = ctx.enter_context(tc.tile_pool(name="consts", bufs=1))
         weights = ctx.enter_context(tc.tile_pool(name="weights", bufs=1))
-        raw_pool = ctx.enter_context(tc.tile_pool(name="raw", bufs=TILES * PREFETCH))
+        raw_pool = ctx.enter_context(tc.tile_pool(name="raw", bufs=PREFETCH))
         stage = ctx.enter_context(tc.tile_pool(name="stage", bufs=2))
         norm = ctx.enter_context(tc.tile_pool(name="norm", bufs=1))
         psum_acc = ctx.enter_context(tc.psum_pool(name="psum_acc", bufs=1))
@@ -61,9 +67,9 @@ def tile_multiheadattn_pb_k_kernel(tc, h_attn, Wo_words, Wo_scales, bo, x, gamma
 
         w_words = []
         w_scales = []
-        for c in range(CHUNKS):
-            words = weights.tile([P, CHUNK * 2 * D], U8, name="w_words%d" % c, align_bytes=64)
-            plane = weights.tile([P, CHUNK * D], U8, name="w_scales%d" % c, align_bytes=64)
+        for c in range(QUADS):
+            words = weights.tile([P, QUAD * 2 * D], U8, name="w_words%d" % c, align_bytes=64)
+            plane = weights.tile([P, QUAD * D], U8, name="w_scales%d" % c, align_bytes=64)
             nc.vector.memset(plane[:].bitcast(I32), 0)
             w_words.append(words)
             w_scales.append(plane)
@@ -88,15 +94,17 @@ def tile_multiheadattn_pb_k_kernel(tc, h_attn, Wo_words, Wo_scales, bo, x, gamma
         batch_tiles = [{} for b in range(BATCH)]
 
         def fetch_weights(c):
-            passes = slice(c * CHUNK, (c + 1) * CHUNK)
-            for r in range(4):
-                nc.sync.dma_start(
-                    out=w_scales[c][r:P:32, :].bitcast(I32).rearrange("q (g n) -> q g n", g=CHUNK),
-                    in_=dram_scales[passes, r:16:4, :].rearrange("g q n -> q g n"),
-                )
+            n = CHUNK_PASSES[c]
+            quad, g0 = divmod(FIRST_PASS[c], QUAD)
+            if g0 == 0:
+                for r in range(4):
+                    nc.sync.dma_start(
+                        out=w_scales[quad][r:P:32, :].bitcast(I32).rearrange("q (g n) -> q g n", g=QUAD),
+                        in_=dram_scales[quad * QUAD : (quad + 1) * QUAD, r:16:4, :].rearrange("g q n -> q g n"),
+                    )
             nc.sync.dma_start(
-                out=w_words[c][:].bitcast(I32).rearrange("p (g n) -> p g n", g=CHUNK),
-                in_=dram_words[passes].rearrange("g p n -> p g n"),
+                out=w_words[quad][:, g0 * 2 * D : (g0 + n) * 2 * D].bitcast(I32).rearrange("p (g n) -> p g n", g=n),
+                in_=dram_words[FIRST_PASS[c] : FIRST_PASS[c] + n].rearrange("g p n -> p g n"),
             )
 
         def fetch(r):
@@ -105,11 +113,15 @@ def tile_multiheadattn_pb_k_kernel(tc, h_attn, Wo_words, Wo_scales, bo, x, gamma
                 nc.sync.dma_start(out=x_sb[:], in_=x.rearrange("b (p t) d -> p b (t d)", t=TILES))
             if r < n_rounds:
                 c, b = rounds[r]
-                by_tile = h_attn[b].rearrange("(p t) k -> t p k", t=TILES)
-                for t in range(TILES):
-                    raw = raw_pool.tile([P, K_CHUNK], BF16)
-                    nc.sync.dma_start(out=raw[:], in_=by_tile[t, :, c * K_CHUNK : (c + 1) * K_CHUNK])
-                    raw_tiles[(r, t)] = raw
+                n = CHUNK_PASSES[c]
+                by_tile = h_attn[b].rearrange("(p t) k -> p t k", t=TILES)[:, :, FIRST_PASS[c] * K_PASS : (FIRST_PASS[c] + n) * K_PASS]
+                raw = raw_pool.tile([P, TILES, n * K_PASS], BF16)
+                if n <= MERGED_PASSES:
+                    nc.sync.dma_start(out=raw[:], in_=by_tile)
+                else:
+                    for t in range(TILES):
+                        nc.sync.dma_start(out=raw[:, t, :], in_=by_tile[:, t, :])
+                raw_tiles[r] = raw
             if 1 <= r <= n_rounds and rounds[r - 1][0] not in fetched_chunks:
                 fetched_chunks.add(rounds[r - 1][0])
                 fetch_weights(rounds[r - 1][0])
@@ -118,37 +130,41 @@ def tile_multiheadattn_pb_k_kernel(tc, h_attn, Wo_words, Wo_scales, bo, x, gamma
                 nc.sync.dma_start(out=beta_sb[:], in_=beta.rearrange("(p t) d -> p (t d)", t=TILES))
 
         def sort_words(r):
-            ordered = stage.tile([P, TILES, CHUNK, HALVES, P], F32)
+            n = CHUNK_PASSES[rounds[r][0]]
+            ordered = stage.tile([P, TILES, n, HALVES, P], F32)
             for t in range(TILES):
                 nc.vector.tensor_copy(
                     out=ordered[:, t],
-                    in_=raw_tiles[(r, t)][:].bitcast(F32).rearrange("r (g p u) -> r g u p", g=CHUNK, u=HALVES),
+                    in_=raw_tiles[r][:, t, :].bitcast(F32).rearrange("r (g p u) -> r g u p", g=n, u=HALVES),
                 )
             ordered_tiles[r] = ordered
 
         def transpose(r):
             ordered = ordered_tiles[r]
-            grouped = stage.tile([P, TILES * CHUNK * P * PACK], BF16, align_bytes=64)
+            n = CHUNK_PASSES[rounds[r][0]]
+            grouped = stage.tile([P, TILES * n * P * PACK], BF16, align_bytes=64)
             grouped_words = grouped[:].bitcast(F32).rearrange(
-                "p (t g r u) -> p t g r u", t=TILES, g=CHUNK, u=HALVES
+                "p (t g r u) -> p t g r u", t=TILES, g=n, u=HALVES
             )
             for t in range(TILES):
-                for g0 in range(0, CHUNK, BANK_PASSES):
+                for g0 in range(0, n, BANK_PASSES):
+                    m = min(BANK_PASSES, n - g0)
                     flipped = psum_work.tile([P, BANK_PASSES, HALVES, P], F32, tag="work")
-                    for g in range(BANK_PASSES):
+                    for g in range(m):
                         for u in range(HALVES):
                             nc.tensor.transpose(flipped[:, g, u, :], ordered[:, t, g0 + g, u, :], identity[:])
                     nc.scalar.copy(
-                        out=grouped_words[:, t, g0 : g0 + BANK_PASSES],
-                        in_=flipped[:].rearrange("p g u r -> p g r u"),
+                        out=grouped_words[:, t, g0 : g0 + m],
+                        in_=flipped[:, 0:m].rearrange("p g u r -> p g r u"),
                     )
             grouped_tiles[r] = grouped
 
         def quantise(r):
             grouped = grouped_tiles[r]
-            codes = stage.tile([P, TILES * CHUNK * P], U32, align_bytes=64)
-            h_scales = stage.tile([P, TILES * CHUNK * P], U8, align_bytes=64)
-            per_tile = CHUNK * P
+            n = CHUNK_PASSES[rounds[r][0]]
+            codes = stage.tile([P, TILES * n * P], U32, align_bytes=64)
+            h_scales = stage.tile([P, TILES * n * P], U8, align_bytes=64)
+            per_tile = n * P
             for t in range(TILES):
                 cols = slice(t * per_tile, (t + 1) * per_tile)
                 nc.vector.quantize_mx(
@@ -161,17 +177,19 @@ def tile_multiheadattn_pb_k_kernel(tc, h_attn, Wo_words, Wo_scales, bo, x, gamma
         def multiply(r):
             c, b = rounds[r]
             codes, h_scales = code_tiles[r]
+            n = CHUNK_PASSES[c]
+            quad, g0 = divmod(FIRST_PASS[c], QUAD)
             for t in range(TILES):
-                for g in range(CHUNK):
-                    tokens = slice((t * CHUNK + g) * P, (t * CHUNK + g + 1) * P)
+                for g in range(n):
+                    tokens = slice((t * n + g) * P, (t * n + g + 1) * P)
                     nc.tensor.matmul_mx(
                         out=acc[b][t][:],
                         lhsT=codes[:, tokens].bitcast(FP8X4),
                         lhsT_scale=h_scales[:, tokens],
-                        rhs=w_words[c][:, g * 2 * D : (g + 1) * 2 * D].bitcast(FP4X4),
-                        rhs_scale=w_scales[c][:, g * D : (g + 1) * D],
+                        rhs=w_words[quad][:, (g0 + g) * 2 * D : (g0 + g + 1) * 2 * D].bitcast(FP4X4),
+                        rhs_scale=w_scales[quad][:, (g0 + g) * D : (g0 + g + 1) * D],
                         start=(c == 0 and g == 0),
-                        stop=(c == CHUNKS - 1 and g == CHUNK - 1),
+                        stop=(c == CHUNKS - 1 and g == n - 1),
                     )
 
         def add_bias_to_residual(b):
@@ -179,7 +197,7 @@ def tile_multiheadattn_pb_k_kernel(tc, h_attn, Wo_words, Wo_scales, bo, x, gamma
             nc.vector.tensor_tensor(out=extra[:], in0=bo_sb[:, b, :], in1=x_sb[:, b, :], op=ALU.add)
             batch_tiles[b]["extra"] = extra
 
-        def sum_and_mean(b):
+        def add_up(b):
             o = norm.tile([P, TILES * D], F32, name="o%d" % b)
             row_sums = norm.tile([P, TILES], F32, name="row_sums%d" % b)
             for t in range(TILES):
@@ -193,16 +211,20 @@ def tile_multiheadattn_pb_k_kernel(tc, h_attn, Wo_words, Wo_scales, bo, x, gamma
                     op1=ALU.add,
                     accum_out=row_sums[:, t : t + 1],
                 )
-            mean_parts = psum_work.tile([P, TILES], F32, tag="work")
-            nc.tensor.matmul(out=mean_parts[:], lhsT=averager[:], rhs=row_sums[:], start=True, stop=True)
-            mean = norm.tile([P, 1], F32, name="mean%d" % b)
-            nc.vector.tensor_reduce(out=mean[:], in_=mean_parts[:], axis=AXIS.X, op=ALU.add)
             batch_tiles[b]["o"] = o
-            batch_tiles[b]["mean"] = mean
+            batch_tiles[b]["row_sums"] = row_sums
+
+        def mean_matmul(b):
+            mean_parts = psum_acc.tile([P, TILES], F32, name="acc%d0" % b)
+            nc.tensor.matmul(
+                out=mean_parts[:], lhsT=averager[:], rhs=batch_tiles[b]["row_sums"][:], start=True, stop=True
+            )
+            batch_tiles[b]["mean_parts"] = mean_parts
 
         def centre(b):
             o = batch_tiles[b]["o"]
-            mean = batch_tiles[b]["mean"]
+            mean = norm.tile([P, 1], F32, name="mean%d" % b)
+            nc.vector.tensor_reduce(out=mean[:], in_=batch_tiles[b]["mean_parts"][:], axis=AXIS.X, op=ALU.add)
             squares = norm.tile([P, TILES * D], F32, name="squares%d" % b)
             square_sums = norm.tile([P, 1], F32, name="square_sums%d" % b)
             nc.scalar.activation(
@@ -212,46 +234,60 @@ def tile_multiheadattn_pb_k_kernel(tc, h_attn, Wo_words, Wo_scales, bo, x, gamma
             nc.vector.scalar_tensor_tensor(
                 out=centred[:], in0=o[:], scalar=mean[:], in1=gamma_sb[:], op0=ALU.subtract, op1=ALU.mult
             )
-            variance = psum_work.tile([P, 1], F32, tag="work")
-            nc.tensor.matmul(out=variance[:], lhsT=averager[:], rhs=square_sums[:], start=True, stop=True)
             batch_tiles[b]["centred"] = centred
-            batch_tiles[b]["variance"] = variance
+            batch_tiles[b]["square_sums"] = square_sums
+
+        def deviation(b):
+            variance = psum_acc.tile([P, 1], F32, name="acc%d1" % b)
+            nc.tensor.matmul(
+                out=variance[:], lhsT=averager[:], rhs=batch_tiles[b]["square_sums"][:], start=True, stop=True
+            )
+            std = norm.tile([P, 1], F32, name="std%d" % b)
+            nc.scalar.activation(out=std[:], in_=variance[:], func=ACT.Sqrt, bias=eps[:])
+            batch_tiles[b]["std"] = std
 
         def normalise_and_store(b):
-            std = norm.tile([P, 1], F32, name="std%d" % b)
-            nc.scalar.activation(out=std[:], in_=batch_tiles[b]["variance"][:], func=ACT.Sqrt, bias=eps[:])
             inv_std = norm.tile([P, 1], F32, name="inv_std%d" % b)
-            nc.vector.reciprocal(out=inv_std[:], in_=std[:])
+            nc.vector.reciprocal(out=inv_std[:], in_=batch_tiles[b]["std"][:])
             result = norm.tile([P, TILES * D], F32, name="result%d" % b)
-            nc.vector.scalar_tensor_tensor(
-                out=result[:],
-                in0=batch_tiles[b]["centred"][:],
-                scalar=inv_std[:],
-                in1=beta_sb[:],
-                op0=ALU.mult,
-                op1=ALU.add,
-            )
-            nc.sync.dma_start(out=out[b].rearrange("(p t) d -> p (t d)", t=TILES), in_=result[:])
+            width = TILES * D // STORE_PIECES
+            for j in range(STORE_PIECES):
+                cols = slice(j * width, (j + 1) * width)
+                nc.vector.scalar_tensor_tensor(
+                    out=result[:, cols],
+                    in0=batch_tiles[b]["centred"][:, cols],
+                    scalar=inv_std[:],
+                    in1=beta_sb[:, cols],
+                    op0=ALU.mult,
+                    op1=ALU.add,
+                )
+                nc.sync.dma_start(out=out[b].rearrange("(p t) d -> p (t d)", t=TILES)[:, cols], in_=result[:, cols])
 
         for r in range(PREFETCH):
             fetch(r)
-        for i in range(n_rounds + 4):
+        for i in range(n_rounds + 2):
             if 0 <= i - 2 < n_rounds:
                 quantise(i - 2)
             if i < n_rounds:
                 sort_words(i)
                 fetch(i + PREFETCH)
-                if rounds[i][0] == CHUNKS - 2:
+                if rounds[i][0] == CHUNKS - LATE:
                     add_bias_to_residual(rounds[i][1])
             if 0 <= i - 1 < n_rounds:
                 transpose(i - 1)
-            for b in range(BATCH):
-                if i == last_round[b] + 4:
-                    centre(b)
-                if i == last_round[b] + 3:
-                    sum_and_mean(b)
+            if i == last_round[0] + 3:
+                add_up(0)
+            if i == last_round[0] + 4:
+                centre(0)
             if 0 <= i - 2 < n_rounds:
                 multiply(i - 2)
-            for b in range(BATCH):
-                if i == last_round[b] + 4:
-                    normalise_and_store(b)
+            if i == last_round[0] + 3:
+                mean_matmul(0)
+            if i == last_round[0] + 4:
+                deviation(0)
+        add_up(1)
+        mean_matmul(1)
+        centre(1)
+        normalise_and_store(0)
+        deviation(1)
+        normalise_and_store(1)

@@ -27,6 +27,7 @@ CHUNKS = len(CHUNK_PASSES)
 FIRST_PASS = [sum(CHUNK_PASSES[:c]) for c in range(CHUNKS)]
 LATE = 2
 STORE_PIECES = 2
+WARM_UP_MATMULS = 8
 QUAD = 4
 QUADS = K // (K_PASS * QUAD)
 MERGED_PASSES = 2
@@ -55,6 +56,12 @@ def tile_multiheadattn_pb_k_kernel(tc, h_attn, Wo_words, Wo_scales, bo, x, gamma
         psum_acc = ctx.enter_context(tc.psum_pool(name="psum_acc", bufs=1))
         psum_work = ctx.enter_context(tc.psum_pool(name="psum_work", bufs=4))
         ctx.enter_context(tc.manual_schedule())
+
+        idle_operand = consts.tile([P, D], BF16)
+        nc.vector.memset(idle_operand[:], 0.0)
+        idle_product = psum_work.tile([P, D], F32, tag="work")
+        for j in range(WARM_UP_MATMULS):
+            nc.tensor.matmul(out=idle_product[:], lhsT=idle_operand[:, 0:P], rhs=idle_operand[:], start=True, stop=True)
 
         identity = consts.tile([P, P], F32)
         masks.make_identity(nc, identity[:])

@@ -70,7 +70,7 @@ def tile_multiheadattn_pb_k_kernel(tc, h_attn, Wo_words, Wo_scales, bo, x, gamma
         eps = consts.tile([P, 1], F32)
         nc.vector.memset(eps[:], LN_EPS)
         warm = consts.tile([P, 1], F32)
-        nc.scalar.activation(out=warm[:], in_=eps[:], func=ACT.Sqrt)
+        nc.scalar.activation(out=warm[:], in_=eps[:], func=ACT.Abs_reciprocal_sqrt)
 
         w_words = []
         w_scales = []
@@ -249,13 +249,12 @@ def tile_multiheadattn_pb_k_kernel(tc, h_attn, Wo_words, Wo_scales, bo, x, gamma
             nc.tensor.matmul(
                 out=variance[:], lhsT=averager[:], rhs=batch_tiles[b]["square_sums"][:], start=True, stop=True
             )
-            std = norm.tile([P, 1], F32, name="std%d" % b)
-            nc.scalar.activation(out=std[:], in_=variance[:], func=ACT.Sqrt, bias=eps[:])
-            batch_tiles[b]["std"] = std
+            inv_std = norm.tile([P, 1], F32, name="inv_std%d" % b)
+            nc.scalar.activation(out=inv_std[:], in_=variance[:], func=ACT.Abs_reciprocal_sqrt, bias=eps[:])
+            batch_tiles[b]["inv_std"] = inv_std
 
         def normalise_and_store(b):
-            inv_std = norm.tile([P, 1], F32, name="inv_std%d" % b)
-            nc.vector.reciprocal(out=inv_std[:], in_=batch_tiles[b]["std"][:])
+            inv_std = batch_tiles[b]["inv_std"]
             result = norm.tile([P, TILES * D], F32, name="result%d" % b)
             width = TILES * D // STORE_PIECES
             for j in range(STORE_PIECES):

@@ -20,20 +20,20 @@ LN_EPS = 1e-5
 P = 128
 PACK = 4
 K_PASS = P * PACK
+PASSES = K // K_PASS
 HALVES = 2
 TILES = SEQ // P
-CHUNK_PASSES = (4,) * 8
+QUAD = 4
+QUADS = PASSES // QUAD
+BANK_PASSES = 2
+HEAD_CHUNKS = 0
+CHUNK_PASSES = (2,) * HEAD_CHUNKS + (4,) * 8
 CHUNKS = len(CHUNK_PASSES)
 FIRST_PASS = [sum(CHUNK_PASSES[:c]) for c in range(CHUNKS)]
 LATE = 2
-STORE_PIECES = 2
 WARM_UP_MATMULS = 8
-QUAD = 4
-QUADS = K // (K_PASS * QUAD)
-MERGED_PASSES = 2
-assert sum(CHUNK_PASSES) * K_PASS == K
-BANK_PASSES = 2
 PREFETCH = 4
+assert sum(CHUNK_PASSES) == PASSES
 
 FLOPS = 2 * BATCH * SEQ * K * D
 
@@ -41,11 +41,16 @@ FLOPS = 2 * BATCH * SEQ * K * D
 def tile_multiheadattn_pb_k_kernel(tc, h_attn, Wo_words, Wo_scales, bo, x, gamma, beta, out):
     nc = tc.nc
 
-    rounds = [(c, b) for c in range(CHUNKS - LATE) for b in range(BATCH)]
-    first_late_round = len(rounds)
-    rounds += [(c, b) for b in range(BATCH) for c in range(CHUNKS - LATE, CHUNKS)]
+    tiles_of = [tuple((b, t) for t in range(TILES)) for b in range(BATCH)]
+    early = range(HEAD_CHUNKS, CHUNKS - LATE)
+    late = range(CHUNKS - LATE, CHUNKS)
+    order = [(tiles_of[0] + tiles_of[1], c) for c in range(HEAD_CHUNKS)]
+    order += [(tiles_of[b], c) for c in early for b in range(BATCH)]
+    order += [(tiles_of[0], c) for c in late]
+    rounds = [(tiles, FIRST_PASS[c], CHUNK_PASSES[c]) for tiles, c in order]
+    rounds += [((tile,), FIRST_PASS[late[0]], PASSES - FIRST_PASS[late[0]]) for tile in tiles_of[1]]
     n_rounds = len(rounds)
-    last_round = [rounds.index((CHUNKS - 1, b)) for b in range(BATCH)]
+    last_round = [len(order) - 1, n_rounds - 1]
 
     with ExitStack() as ctx:
         consts = ctx.enter_context(tc.tile_pool(name="consts", bufs=1))
@@ -67,8 +72,12 @@ def tile_multiheadattn_pb_k_kernel(tc, h_attn, Wo_words, Wo_scales, bo, x, gamma
         masks.make_identity(nc, identity[:])
         averager = consts.tile([P, P], F32)
         nc.vector.memset(averager[:], 1.0 / (SEQ * D))
+        tile_averager = consts.tile([P, P], F32)
+        nc.vector.memset(tile_averager[:], 1.0 / (P * D))
         eps = consts.tile([P, 1], F32)
         nc.vector.memset(eps[:], LN_EPS)
+        zero = consts.tile([P, 1], F32)
+        nc.vector.memset(zero[:], 0.0)
         warm = consts.tile([P, 1], F32)
         nc.scalar.activation(out=warm[:], in_=eps[:], func=ACT.Abs_reciprocal_sqrt)
 
@@ -88,21 +97,20 @@ def tile_multiheadattn_pb_k_kernel(tc, h_attn, Wo_words, Wo_scales, bo, x, gamma
             for b in range(BATCH)
         ]
 
-        bo_sb = norm.tile([P, BATCH, TILES * D], BF16)
-        x_sb = norm.tile([P, BATCH, TILES * D], BF16)
-        gamma_sb = norm.tile([P, TILES * D], BF16)
-        beta_sb = norm.tile([P, TILES * D], BF16)
+        bo_sb = norm.tile([P, BATCH, TILES, D], BF16)
+        x_sb = norm.tile([P, BATCH, TILES, D], BF16)
+        gamma_sb = norm.tile([P, TILES, D], BF16)
+        beta_sb = norm.tile([P, TILES, D], BF16)
 
         raw_tiles = {}
         ordered_tiles = {}
         grouped_tiles = {}
         code_tiles = {}
-        fetched_chunks = set()
-        batch_tiles = [{} for b in range(BATCH)]
+        fetched = set()
+        parts = [{} for b in range(BATCH)]
 
-        def fetch_weights(c):
-            n = CHUNK_PASSES[c]
-            quad, g0 = divmod(FIRST_PASS[c], QUAD)
+        def fetch_weights(first, n):
+            quad, g0 = divmod(first, QUAD)
             if g0 == 0:
                 for r in range(4):
                     nc.sync.dma_start(
@@ -111,189 +119,228 @@ def tile_multiheadattn_pb_k_kernel(tc, h_attn, Wo_words, Wo_scales, bo, x, gamma
                     )
             nc.sync.dma_start(
                 out=w_words[quad][:, g0 * 2 * D : (g0 + n) * 2 * D].bitcast(I32).rearrange("p (g n) -> p g n", g=n),
-                in_=dram_words[FIRST_PASS[c] : FIRST_PASS[c] + n].rearrange("g p n -> p g n"),
+                in_=dram_words[first : first + n].rearrange("g p n -> p g n"),
             )
 
+        def load_norm(tile, source):
+            nc.sync.dma_start(out=tile, in_=source.rearrange("(p t) d -> p t d", t=TILES))
+
         def fetch(r):
-            if r == first_late_round:
-                nc.sync.dma_start(out=bo_sb[:], in_=bo.rearrange("b (p t) d -> p b (t d)", t=TILES))
-                nc.sync.dma_start(out=x_sb[:], in_=x.rearrange("b (p t) d -> p b (t d)", t=TILES))
             if r < n_rounds:
-                c, b = rounds[r]
-                n = CHUNK_PASSES[c]
-                by_tile = h_attn[b].rearrange("(p t) k -> p t k", t=TILES)[:, :, FIRST_PASS[c] * K_PASS : (FIRST_PASS[c] + n) * K_PASS]
-                raw = raw_pool.tile([P, TILES, n * K_PASS], BF16)
-                if n <= MERGED_PASSES:
-                    nc.sync.dma_start(out=raw[:], in_=by_tile)
-                else:
-                    for t in range(TILES):
-                        nc.sync.dma_start(out=raw[:, t, :], in_=by_tile[:, t, :])
+                tiles, first, n = rounds[r]
+                raw = raw_pool.tile([P, len(tiles), n * K_PASS], BF16)
+                together = TILES if n <= BANK_PASSES else 1
+                m = min(n, QUAD)
+                for j in range(0, len(tiles), together):
+                    b, t = tiles[j]
+                    for g in range(0, n, m):
+                        nc.sync.dma_start(
+                            out=raw[:, j : j + together, g * K_PASS : (g + m) * K_PASS],
+                            in_=h_attn[b].rearrange("(p t) k -> p t k", t=TILES)[
+                                :, t : t + together, (first + g) * K_PASS : (first + g + m) * K_PASS
+                            ],
+                        )
                 raw_tiles[r] = raw
-            if 1 <= r <= n_rounds and rounds[r - 1][0] not in fetched_chunks:
-                fetched_chunks.add(rounds[r - 1][0])
-                fetch_weights(rounds[r - 1][0])
+            if 1 <= r <= n_rounds and rounds[r - 1][1] not in fetched:
+                fetched.add(rounds[r - 1][1])
+                fetch_weights(rounds[r - 1][1], rounds[r - 1][2])
+            if r == last_round[0] - 1:
+                load_norm(bo_sb[:, 0], bo[0])
+                load_norm(x_sb[:, 0], x[0])
             if r == n_rounds - 1:
-                nc.sync.dma_start(out=gamma_sb[:], in_=gamma.rearrange("(p t) d -> p (t d)", t=TILES))
-                nc.sync.dma_start(out=beta_sb[:], in_=beta.rearrange("(p t) d -> p (t d)", t=TILES))
+                load_norm(bo_sb[:, 1], bo[1])
+                load_norm(x_sb[:, 1], x[1])
+            if r == n_rounds - 1:
+                load_norm(gamma_sb[:], gamma)
+                load_norm(beta_sb[:], beta)
 
         def sort_words(r):
-            n = CHUNK_PASSES[rounds[r][0]]
-            ordered = stage.tile([P, TILES, n, HALVES, P], F32)
-            for t in range(TILES):
-                nc.vector.tensor_copy(
-                    out=ordered[:, t],
-                    in_=raw_tiles[r][:, t, :].bitcast(F32).rearrange("r (g p u) -> r g u p", g=n, u=HALVES),
-                )
+            tiles, first, n = rounds[r]
+            ordered = stage.tile([P, len(tiles), n, HALVES, P], F32)
+            m = min(n, QUAD)
+            for j in range(len(tiles)):
+                view = raw_tiles[r][:, j, :].bitcast(F32).rearrange("r (g p u) -> r g u p", g=n, u=HALVES)
+                for g in range(0, n, m):
+                    nc.vector.tensor_copy(out=ordered[:, j, g : g + m], in_=view[:, g : g + m])
             ordered_tiles[r] = ordered
 
         def transpose(r):
             ordered = ordered_tiles[r]
-            n = CHUNK_PASSES[rounds[r][0]]
-            grouped = stage.tile([P, TILES * n * P * PACK], BF16, align_bytes=64)
+            tiles, first, n = rounds[r]
+            grouped = stage.tile([P, len(tiles) * n * P * PACK], BF16, align_bytes=64)
             grouped_words = grouped[:].bitcast(F32).rearrange(
-                "p (t g r u) -> p t g r u", t=TILES, g=n, u=HALVES
+                "p (j g r u) -> p j g r u", j=len(tiles), g=n, u=HALVES
             )
-            for t in range(TILES):
+            for j in range(len(tiles)):
                 for g0 in range(0, n, BANK_PASSES):
-                    m = min(BANK_PASSES, n - g0)
                     flipped = psum_work.tile([P, BANK_PASSES, HALVES, P], F32, tag="work")
-                    for g in range(m):
+                    for g in range(BANK_PASSES):
                         for u in range(HALVES):
-                            nc.tensor.transpose(flipped[:, g, u, :], ordered[:, t, g0 + g, u, :], identity[:])
+                            nc.tensor.transpose(flipped[:, g, u, :], ordered[:, j, g0 + g, u, :], identity[:])
                     nc.scalar.copy(
-                        out=grouped_words[:, t, g0 : g0 + m],
-                        in_=flipped[:, 0:m].rearrange("p g u r -> p g r u"),
+                        out=grouped_words[:, j, g0 : g0 + BANK_PASSES],
+                        in_=flipped[:].rearrange("p g u r -> p g r u"),
                     )
             grouped_tiles[r] = grouped
 
         def quantise(r):
             grouped = grouped_tiles[r]
-            n = CHUNK_PASSES[rounds[r][0]]
-            codes = stage.tile([P, TILES * n * P], U32, align_bytes=64)
-            h_scales = stage.tile([P, TILES * n * P], U8, align_bytes=64)
-            per_tile = n * P
-            for t in range(TILES):
-                cols = slice(t * per_tile, (t + 1) * per_tile)
+            tiles, first, n = rounds[r]
+            codes = stage.tile([P, len(tiles) * n * P], U32, align_bytes=64)
+            h_scales = stage.tile([P, len(tiles) * n * P], U8, align_bytes=64)
+            step = min(n, QUAD) * P
+            for first_col in range(0, len(tiles) * n * P, step):
+                cols = slice(first_col, first_col + step)
                 nc.vector.quantize_mx(
                     out=codes[:, cols].bitcast(FP8X4),
                     scales=h_scales[:, cols],
-                    in_=grouped[:, t * per_tile * PACK : (t + 1) * per_tile * PACK],
+                    in_=grouped[:, first_col * PACK : (first_col + step) * PACK],
                 )
             code_tiles[r] = (codes, h_scales)
 
-        def multiply(r):
-            c, b = rounds[r]
+        def multiply(r, passes=None):
+            tiles, first, n = rounds[r]
             codes, h_scales = code_tiles[r]
-            n = CHUNK_PASSES[c]
-            quad, g0 = divmod(FIRST_PASS[c], QUAD)
-            for t in range(TILES):
-                for g in range(n):
-                    tokens = slice((t * n + g) * P, (t * n + g + 1) * P)
+            for j, (b, t) in enumerate(tiles):
+                for g in passes or range(n):
+                    quad, slot = divmod(first + g, QUAD)
+                    tokens = slice((j * n + g) * P, (j * n + g + 1) * P)
                     nc.tensor.matmul_mx(
                         out=acc[b][t][:],
                         lhsT=codes[:, tokens].bitcast(FP8X4),
                         lhsT_scale=h_scales[:, tokens],
-                        rhs=w_words[quad][:, (g0 + g) * 2 * D : (g0 + g + 1) * 2 * D].bitcast(FP4X4),
-                        rhs_scale=w_scales[quad][:, (g0 + g) * D : (g0 + g + 1) * D],
-                        start=(c == 0 and g == 0),
-                        stop=(c == CHUNKS - 1 and g == n - 1),
+                        rhs=w_words[quad][:, slot * 2 * D : (slot + 1) * 2 * D].bitcast(FP4X4),
+                        rhs_scale=w_scales[quad][:, slot * D : (slot + 1) * D],
+                        start=(first + g == 0),
+                        stop=(first + g == PASSES - 1),
                     )
 
         def add_bias_to_residual(b):
             extra = norm.tile([P, TILES * D], F32, name="extra%d" % b)
-            nc.vector.tensor_tensor(out=extra[:], in0=bo_sb[:, b, :], in1=x_sb[:, b, :], op=ALU.add)
-            batch_tiles[b]["extra"] = extra
-
-        def add_up(b):
-            o = norm.tile([P, TILES * D], F32, name="o%d" % b)
-            row_sums = norm.tile([P, TILES], F32, name="row_sums%d" % b)
-            for t in range(TILES):
-                cols = slice(t * D, (t + 1) * D)
-                nc.vector.scalar_tensor_tensor(
-                    out=o[:, cols],
-                    in0=acc[b][t][:],
-                    scalar=1.0,
-                    in1=batch_tiles[b]["extra"][:, cols],
-                    op0=ALU.mult,
-                    op1=ALU.add,
-                    accum_out=row_sums[:, t : t + 1],
-                )
-            batch_tiles[b]["o"] = o
-            batch_tiles[b]["row_sums"] = row_sums
-
-        def mean_matmul(b):
-            mean_parts = psum_acc.tile([P, TILES], F32, name="acc%d0" % b)
-            nc.tensor.matmul(
-                out=mean_parts[:], lhsT=averager[:], rhs=batch_tiles[b]["row_sums"][:], start=True, stop=True
+            nc.vector.tensor_tensor(
+                out=extra[:],
+                in0=bo_sb[:, b].rearrange("p t d -> p (t d)"),
+                in1=x_sb[:, b].rearrange("p t d -> p (t d)"),
+                op=ALU.add,
             )
-            batch_tiles[b]["mean_parts"] = mean_parts
+            parts[b]["extra"] = extra
 
-        def centre(b):
-            o = batch_tiles[b]["o"]
-            mean = norm.tile([P, 1], F32, name="mean%d" % b)
-            nc.vector.tensor_reduce(out=mean[:], in_=batch_tiles[b]["mean_parts"][:], axis=AXIS.X, op=ALU.add)
-            squares = norm.tile([P, TILES * D], F32, name="squares%d" % b)
-            square_sums = norm.tile([P, 1], F32, name="square_sums%d" % b)
-            nc.scalar.activation(
-                out=squares[:], in_=o[:], func=ACT.Square, bias=mean[:], scale=-1.0, accum_out=square_sums[:]
-            )
-            centred = norm.tile([P, TILES * D], F32, name="centred%d" % b)
+        def add_up(b, t, shift=None):
+            o = norm.tile([P, D], F32, name="o%d%d" % (b, t))
+            row_sum = norm.tile([P, 1], F32, name="row_sum%d%d" % (b, t))
             nc.vector.scalar_tensor_tensor(
-                out=centred[:], in0=o[:], scalar=mean[:], in1=gamma_sb[:], op0=ALU.subtract, op1=ALU.mult
+                out=o[:],
+                in0=acc[b][t][:],
+                scalar=0.0 if shift is None else shift,
+                in1=parts[b]["extra"][:, t * D : (t + 1) * D],
+                op0=ALU.subtract,
+                op1=ALU.add,
+                accum_out=row_sum[:],
             )
-            batch_tiles[b]["centred"] = centred
-            batch_tiles[b]["square_sums"] = square_sums
+            parts[b]["o", t] = o
+            parts[b]["row_sum", t] = row_sum
 
-        def deviation(b):
-            variance = psum_acc.tile([P, 1], F32, name="acc%d1" % b)
-            nc.tensor.matmul(
-                out=variance[:], lhsT=averager[:], rhs=batch_tiles[b]["square_sums"][:], start=True, stop=True
+        def sum_squares(b, t, bias):
+            square = norm.tile([P, D], F32, name="square")
+            square_sum = norm.tile([P, 1], F32, name="square_sum%d%d" % (b, t))
+            nc.scalar.activation(
+                out=square[:], in_=parts[b]["o", t][:], func=ACT.Square, bias=bias, scale=-1.0, accum_out=square_sum[:]
             )
-            inv_std = norm.tile([P, 1], F32, name="inv_std%d" % b)
-            nc.scalar.activation(out=inv_std[:], in_=variance[:], func=ACT.Abs_reciprocal_sqrt, bias=eps[:])
-            batch_tiles[b]["inv_std"] = inv_std
+            parts[b]["square_sum", t] = square_sum
 
-        def normalise_and_store(b):
-            inv_std = batch_tiles[b]["inv_std"]
-            result = norm.tile([P, TILES * D], F32, name="result%d" % b)
-            width = TILES * D // STORE_PIECES
-            for j in range(STORE_PIECES):
-                cols = slice(j * width, (j + 1) * width)
-                nc.vector.scalar_tensor_tensor(
-                    out=result[:, cols],
-                    in0=batch_tiles[b]["centred"][:, cols],
-                    scalar=inv_std[:],
-                    in1=beta_sb[:, cols],
-                    op0=ALU.mult,
-                    op1=ALU.add,
+        def average(bank, matrix, columns):
+            result = psum_acc.tile([P, 1], F32, name=bank)
+            for j, column in enumerate(columns):
+                nc.tensor.matmul(
+                    out=result[:], lhsT=matrix[:], rhs=column[:], start=(j == 0), stop=(j == len(columns) - 1)
                 )
-                nc.sync.dma_start(out=out[b].rearrange("(p t) d -> p (t d)", t=TILES)[:, cols], in_=result[:, cols])
+            return result
+
+        def to_sbuf(name, value):
+            copy = norm.tile([P, 1], F32, name=name)
+            nc.vector.tensor_copy(out=copy[:], in_=value[:])
+            return copy
+
+        def scale_by_gamma(b, t, mean):
+            centred = norm.tile([P, D], F32, name="centred%d%d" % (b, t))
+            nc.vector.scalar_tensor_tensor(
+                out=centred[:],
+                in0=parts[b]["o", t][:],
+                scalar=mean,
+                in1=gamma_sb[:, t, :],
+                op0=ALU.subtract,
+                op1=ALU.mult,
+            )
+            parts[b]["centred", t] = centred
+
+        def invert(b, variance, offset):
+            inv_std = norm.tile([P, 1], F32, name="inv_std%d" % b)
+            nc.scalar.activation(out=inv_std[:], in_=variance[:], func=ACT.Abs_reciprocal_sqrt, bias=offset)
+            parts[b]["inv_std"] = inv_std
+
+        def normalise_and_store(b, t):
+            result = norm.tile([P, D], F32, name="result%d%d" % (b, t))
+            nc.vector.scalar_tensor_tensor(
+                out=result[:],
+                in0=parts[b]["centred", t][:],
+                scalar=parts[b]["inv_std"][:],
+                in1=beta_sb[:, t, :],
+                op0=ALU.mult,
+                op1=ALU.add,
+            )
+            nc.sync.dma_start(out=out[b].rearrange("(p t) d -> p t d", t=TILES)[:, t, :], in_=result[:])
 
         for r in range(PREFETCH):
             fetch(r)
-        for i in range(n_rounds + 2):
-            if 0 <= i - 2 < n_rounds:
+        for i in range(n_rounds + 1):
+            if i - 2 >= 0:
                 quantise(i - 2)
             if i < n_rounds:
                 sort_words(i)
                 fetch(i + PREFETCH)
-                if rounds[i][0] == CHUNKS - LATE:
-                    add_bias_to_residual(rounds[i][1])
-            if 0 <= i - 1 < n_rounds:
+            if i == last_round[0] - 1:
+                add_bias_to_residual(0)
+            if i == n_rounds:
+                add_bias_to_residual(1)
+            if i - 1 >= 0:
                 transpose(i - 1)
-            if i == last_round[0] + 3:
-                add_up(0)
-            if i == last_round[0] + 4:
-                centre(0)
-            if 0 <= i - 2 < n_rounds:
+            if i - 2 >= 0 and i < n_rounds:
                 multiply(i - 2)
-            if i == last_round[0] + 3:
-                mean_matmul(0)
-            if i == last_round[0] + 4:
-                deviation(0)
-        add_up(1)
-        mean_matmul(1)
-        centre(1)
-        normalise_and_store(0)
-        deviation(1)
-        normalise_and_store(1)
+        last = n_rounds - 1
+        for t in range(TILES):
+            add_up(0, t)
+        multiply(last - 1)
+        zero_mean = average("acc00", averager, (parts[0]["row_sum", 0], parts[0]["row_sum", 1]))
+        quantise(last)
+        multiply(last, range(6))
+        mean = to_sbuf("mean0", zero_mean)
+        for t in range(TILES):
+            sum_squares(0, t, mean[:])
+        add_up(1, 0)
+        for t in range(TILES):
+            scale_by_gamma(0, t, mean[:])
+        shift_sum = average("acc10", tile_averager, (parts[1]["row_sum", 0],))
+        multiply(last, range(6, 8))
+        variance = average("acc01", averager, (parts[0]["square_sum", 0], parts[0]["square_sum", 1]))
+        invert(0, variance, eps[:])
+        shift = to_sbuf("shift", shift_sum)
+        sum_squares(1, 0, shift[:])
+        add_up(1, 1, shift[:])
+        delta = average("acc00", averager, (parts[1]["row_sum", 1],))
+        sum_squares(1, 1, zero[:])
+        normalise_and_store(0, 0)
+        minus_delta = norm.tile([P, 1], F32)
+        nc.vector.tensor_scalar(out=minus_delta[:], in0=delta[:], scalar1=-1.0, scalar2=None, op0=ALU.mult)
+        mean = norm.tile([P, 1], F32, name="mean1")
+        nc.vector.tensor_tensor(out=mean[:], in0=delta[:], in1=shift[:], op=ALU.add)
+        scale_by_gamma(1, 1, delta[:])
+        offset = norm.tile([P, 1], F32)
+        nc.vector.scalar_tensor_tensor(
+            out=offset[:], in0=delta[:], scalar=minus_delta[:], in1=eps[:], op0=ALU.mult, op1=ALU.add
+        )
+        spread = average("acc11", averager, (parts[1]["square_sum", 0], parts[1]["square_sum", 1]))
+        invert(1, spread, offset[:])
+        scale_by_gamma(1, 0, mean[:])
+        normalise_and_store(0, 1)
+        for t in range(TILES):
+            normalise_and_store(1, t)

@@ -154,6 +154,9 @@ def tile_multiheadattn_pb_k_kernel(tc, h_attn, Wo_words, Wo_scales, bo, x, gamma
                 load_norm(gamma_sb[:], gamma)
                 load_norm(beta_sb[:], beta)
 
+        def scalar_share(r):
+            return 2 if r == n_rounds - 1 else 0
+
         def sort_words(r):
             tiles, first, n = rounds[r]
             ordered = stage.tile([P, len(tiles), n, HALVES, P], F32)
@@ -161,8 +164,17 @@ def tile_multiheadattn_pb_k_kernel(tc, h_attn, Wo_words, Wo_scales, bo, x, gamma
             for j in range(len(tiles)):
                 view = raw_tiles[r][:, j, :].bitcast(F32).rearrange("r (g p u) -> r g u p", g=n, u=HALVES)
                 for g in range(0, n, m):
-                    nc.vector.tensor_copy(out=ordered[:, j, g : g + m], in_=view[:, g : g + m])
+                    mine = m - scalar_share(r) if (j, g + m) == (len(tiles) - 1, n) else m
+                    nc.vector.tensor_copy(out=ordered[:, j, g : g + mine], in_=view[:, g : g + mine])
             ordered_tiles[r] = ordered
+
+        def sort_rest(r):
+            tiles, first, n = rounds[r]
+            j = len(tiles) - 1
+            g = n - scalar_share(r)
+            if g < n:
+                view = raw_tiles[r][:, j, :].bitcast(F32).rearrange("r (g p u) -> r g u p", g=n, u=HALVES)
+                nc.scalar.copy(out=ordered_tiles[r][:, j, g:n], in_=view[:, g:n])
 
         def transpose(r):
             ordered = ordered_tiles[r]
@@ -273,9 +285,11 @@ def tile_multiheadattn_pb_k_kernel(tc, h_attn, Wo_words, Wo_scales, bo, x, gamma
             )
             parts[b]["centred", t] = centred
 
-        def invert(b, variance, offset):
+        def invert(b, variance, offset, sign=1.0):
             inv_std = norm.tile([P, 1], F32, name="inv_std%d" % b)
-            nc.scalar.activation(out=inv_std[:], in_=variance[:], func=ACT.Abs_reciprocal_sqrt, bias=offset)
+            nc.scalar.activation(
+                out=inv_std[:], in_=variance[:], func=ACT.Abs_reciprocal_sqrt, bias=offset, scale=sign
+            )
             parts[b]["inv_std"] = inv_std
 
         def normalise_and_store(b, t):
@@ -297,13 +311,15 @@ def tile_multiheadattn_pb_k_kernel(tc, h_attn, Wo_words, Wo_scales, bo, x, gamma
                 quantise(i - 2)
             if i < n_rounds:
                 sort_words(i)
-                fetch(i + PREFETCH)
             if i == last_round[0] - 1:
                 add_bias_to_residual(0)
             if i == n_rounds:
                 add_bias_to_residual(1)
             if i - 1 >= 0:
                 transpose(i - 1)
+            if i < n_rounds:
+                sort_rest(i)
+                fetch(i + PREFETCH)
             if i - 2 >= 0 and i < n_rounds:
                 multiply(i - 2)
         last = n_rounds - 1
@@ -322,24 +338,22 @@ def tile_multiheadattn_pb_k_kernel(tc, h_attn, Wo_words, Wo_scales, bo, x, gamma
         shift_sum = average("acc10", tile_averager, (parts[1]["row_sum", 0],))
         multiply(last, range(6, 8))
         variance = average("acc01", averager, (parts[0]["square_sum", 0], parts[0]["square_sum", 1]))
-        invert(0, variance, eps[:])
         shift = to_sbuf("shift", shift_sum)
         sum_squares(1, 0, shift[:])
+        invert(0, variance, eps[:])
         add_up(1, 1, shift[:])
         delta = average("acc00", averager, (parts[1]["row_sum", 1],))
         sum_squares(1, 1, zero[:])
         normalise_and_store(0, 0)
-        minus_delta = norm.tile([P, 1], F32)
-        nc.vector.tensor_scalar(out=minus_delta[:], in0=delta[:], scalar1=-1.0, scalar2=None, op0=ALU.mult)
         mean = norm.tile([P, 1], F32, name="mean1")
         nc.vector.tensor_tensor(out=mean[:], in0=delta[:], in1=shift[:], op=ALU.add)
         scale_by_gamma(1, 1, delta[:])
         offset = norm.tile([P, 1], F32)
         nc.vector.scalar_tensor_tensor(
-            out=offset[:], in0=delta[:], scalar=minus_delta[:], in1=eps[:], op0=ALU.mult, op1=ALU.add
+            out=offset[:], in0=delta[:], scalar=delta[:], in1=eps[:], op0=ALU.mult, op1=ALU.subtract
         )
         spread = average("acc11", averager, (parts[1]["square_sum", 0], parts[1]["square_sum", 1]))
-        invert(1, spread, offset[:])
+        invert(1, spread, offset[:], -1.0)
         scale_by_gamma(1, 0, mean[:])
         normalise_and_store(0, 1)
         for t in range(TILES):

@@ -92,10 +92,7 @@ def tile_multiheadattn_pb_k_kernel(tc, h_attn, Wo_words, Wo_scales, bo, x, gamma
         dram_words = Wo_words.bitcast(I32)
         dram_scales = Wo_scales.bitcast(I32)
 
-        acc = [
-            [psum_acc.tile([P, D], F32, name="acc%d%d" % (b, t)) for t in range(TILES)]
-            for b in range(BATCH)
-        ]
+        acc = [[None] * TILES for b in range(BATCH)]
 
         bo_sb = norm.tile([P, BATCH, TILES, D], BF16)
         x_sb = norm.tile([P, BATCH, TILES, D], BF16)
@@ -185,7 +182,10 @@ def tile_multiheadattn_pb_k_kernel(tc, h_attn, Wo_words, Wo_scales, bo, x, gamma
             )
             for j in range(len(tiles)):
                 for g0 in range(0, n, BANK_PASSES):
-                    flipped = psum_work.tile([P, BANK_PASSES, HALVES, P], F32, tag="work")
+                    if (r, j) == (1, TILES - 1):
+                        flipped = psum_acc.tile([P, BANK_PASSES, HALVES, P], F32, name="acc1%d" % (g0 // BANK_PASSES))
+                    else:
+                        flipped = psum_work.tile([P, BANK_PASSES, HALVES, P], F32, tag="work")
                     for g in range(BANK_PASSES):
                         for u in range(HALVES):
                             nc.tensor.transpose(flipped[:, g, u, :], ordered[:, j, g0 + g, u, :], identity[:])
@@ -214,6 +214,8 @@ def tile_multiheadattn_pb_k_kernel(tc, h_attn, Wo_words, Wo_scales, bo, x, gamma
             tiles, first, n = rounds[r]
             codes, h_scales = code_tiles[r]
             for j, (b, t) in enumerate(tiles):
+                if first == 0:
+                    acc[b][t] = psum_acc.tile([P, D], F32, name="acc%d%d" % (b, t))
                 for g in passes or range(n):
                     quad, slot = divmod(first + g, QUAD)
                     tokens = slice((j * n + g) * P, (j * n + g + 1) * P)
@@ -253,7 +255,7 @@ def tile_multiheadattn_pb_k_kernel(tc, h_attn, Wo_words, Wo_scales, bo, x, gamma
             parts[b]["row_sum", t] = row_sum
 
         def sum_squares(b, t, bias):
-            square = norm.tile([P, D], F32, name="square")
+            square = norm.tile([P, D], F32, name="square%d%d" % (b, t))
             square_sum = norm.tile([P, 1], F32, name="square_sum%d%d" % (b, t))
             nc.scalar.activation(
                 out=square[:], in_=parts[b]["o", t][:], func=ACT.Square, bias=bias, scale=-1.0, accum_out=square_sum[:]
@@ -292,17 +294,21 @@ def tile_multiheadattn_pb_k_kernel(tc, h_attn, Wo_words, Wo_scales, bo, x, gamma
             )
             parts[b]["inv_std"] = inv_std
 
-        def normalise_and_store(b, t):
+        def normalise_and_store(b, t, pieces=1):
             result = norm.tile([P, D], F32, name="result%d%d" % (b, t))
-            nc.vector.scalar_tensor_tensor(
-                out=result[:],
-                in0=parts[b]["centred", t][:],
-                scalar=parts[b]["inv_std"][:],
-                in1=beta_sb[:, t, :],
-                op0=ALU.mult,
-                op1=ALU.add,
-            )
-            nc.sync.dma_start(out=out[b].rearrange("(p t) d -> p t d", t=TILES)[:, t, :], in_=result[:])
+            for j in range(pieces):
+                cols = slice(j * D // pieces, (j + 1) * D // pieces)
+                nc.vector.scalar_tensor_tensor(
+                    out=result[:, cols],
+                    in0=parts[b]["centred", t][:, cols],
+                    scalar=parts[b]["inv_std"][:],
+                    in1=beta_sb[:, t, cols],
+                    op0=ALU.mult,
+                    op1=ALU.add,
+                )
+                nc.sync.dma_start(
+                    out=out[b].rearrange("(p t) d -> p t d", t=TILES)[:, t, cols], in_=result[:, cols]
+                )
 
         for r in range(PREFETCH):
             fetch(r)
@@ -357,4 +363,4 @@ def tile_multiheadattn_pb_k_kernel(tc, h_attn, Wo_words, Wo_scales, bo, x, gamma
         scale_by_gamma(1, 0, mean[:])
         normalise_and_store(0, 1)
         for t in range(TILES):
-            normalise_and_store(1, t)
+            normalise_and_store(1, t, 2)

from contextlib import ExitStack

import concourse.masks as masks
import concourse.mybir as mybir

F32 = mybir.dt.float32
BF16 = mybir.dt.bfloat16
I32 = mybir.dt.int32
U32 = mybir.dt.uint32
U8 = mybir.dt.uint8
FP8X4 = mybir.dt.float8_e4m3fn_x4
FP4X4 = mybir.dt.float4_e2m1fn_x4
ALU = mybir.AluOpType
ACT = mybir.ActivationFunctionType
AXIS = mybir.AxisListType

BATCH, SEQ, D, K = 2, 256, 512, 16384
LN_EPS = 1e-5

P = 128
PACK = 4
K_PASS = P * PACK
PASSES = K // K_PASS
HALVES = 2
TILES = SEQ // P
QUAD = 4
QUADS = PASSES // QUAD
BANK_PASSES = 2
HEAD_CHUNKS = 0
CHUNK_PASSES = (2,) * HEAD_CHUNKS + (4,) * 8
CHUNKS = len(CHUNK_PASSES)
FIRST_PASS = [sum(CHUNK_PASSES[:c]) for c in range(CHUNKS)]
LATE = 2
WARM_UP_MATMULS = 8
PREFETCH = 4
assert sum(CHUNK_PASSES) == PASSES

FLOPS = 2 * BATCH * SEQ * K * D


def tile_multiheadattn_pb_k_kernel(tc, h_attn, Wo_words, Wo_scales, bo, x, gamma, beta, out):
    nc = tc.nc

    tiles_of = [tuple((b, t) for t in range(TILES)) for b in range(BATCH)]
    early = range(HEAD_CHUNKS, CHUNKS - LATE)
    late = range(CHUNKS - LATE, CHUNKS)
    order = [(tiles_of[0] + tiles_of[1], c) for c in range(HEAD_CHUNKS)]
    order += [(tiles_of[b], c) for c in early for b in range(BATCH)]
    order += [(tiles_of[0], c) for c in late]
    rounds = [(tiles, FIRST_PASS[c], CHUNK_PASSES[c]) for tiles, c in order]
    rounds += [((tile,), FIRST_PASS[late[0]], PASSES - FIRST_PASS[late[0]]) for tile in tiles_of[1]]
    n_rounds = len(rounds)
    last_round = [len(order) - 1, n_rounds - 1]

    with ExitStack() as ctx:
        consts = ctx.enter_context(tc.tile_pool(name="consts", bufs=1))
        weights = ctx.enter_context(tc.tile_pool(name="weights", bufs=1))
        raw_pool = ctx.enter_context(tc.tile_pool(name="raw", bufs=PREFETCH))
        stage = ctx.enter_context(tc.tile_pool(name="stage", bufs=2))
        norm = ctx.enter_context(tc.tile_pool(name="norm", bufs=1))
        psum_acc = ctx.enter_context(tc.psum_pool(name="psum_acc", bufs=1))
        psum_work = ctx.enter_context(tc.psum_pool(name="psum_work", bufs=4))
        ctx.enter_context(tc.manual_schedule())

        idle_operand = consts.tile([P, D], BF16)
        nc.vector.memset(idle_operand[:], 0.0)
        idle_product = psum_work.tile([P, D], F32, tag="work")
        for j in range(WARM_UP_MATMULS):
            nc.tensor.matmul(out=idle_product[:], lhsT=idle_operand[:, 0:P], rhs=idle_operand[:], start=True, stop=True)

        identity = consts.tile([P, P], F32)
        masks.make_identity(nc, identity[:])
        averager = consts.tile([P, P], F32)
        nc.vector.memset(averager[:], 1.0 / (SEQ * D))
        tile_averager = consts.tile([P, P], F32)
        nc.vector.memset(tile_averager[:], 1.0 / (P * D))
        eps = consts.tile([P, 1], F32)
        nc.vector.memset(eps[:], LN_EPS)
        zero = consts.tile([P, 1], F32)
        nc.vector.memset(zero[:], 0.0)
        warm = consts.tile([P, 1], F32)
        nc.scalar.activation(out=warm[:], in_=eps[:], func=ACT.Abs_reciprocal_sqrt)

        w_words = []
        w_scales = []
        for c in range(QUADS):
            words = weights.tile([P, QUAD * 2 * D], U8, name="w_words%d" % c, align_bytes=64)
            plane = weights.tile([P, QUAD * D], U8, name="w_scales%d" % c, align_bytes=64)
            nc.vector.memset(plane[:].bitcast(I32), 0)
            w_words.append(words)
            w_scales.append(plane)
        dram_words = Wo_words.bitcast(I32)
        dram_scales = Wo_scales.bitcast(I32)

        acc = [[None] * TILES for b in range(BATCH)]

        bo_sb = norm.tile([P, BATCH, TILES, D], BF16)
        x_sb = norm.tile([P, BATCH, TILES, D], BF16)
        gamma_sb = norm.tile([P, TILES, D], BF16)
        beta_sb = norm.tile([P, TILES, D], BF16)

        raw_tiles = {}
        ordered_tiles = {}
        grouped_tiles = {}
        code_tiles = {}
        fetched = set()
        parts = [{} for b in range(BATCH)]

        def fetch_weights(first, n):
            quad, g0 = divmod(first, QUAD)
            if g0 == 0:
                for r in range(4):
                    nc.sync.dma_start(
                        out=w_scales[quad][r:P:32, :].bitcast(I32).rearrange("q (g n) -> q g n", g=QUAD),
                        in_=dram_scales[quad * QUAD : (quad + 1) * QUAD, r:16:4, :].rearrange("g q n -> q g n"),
                    )
            nc.sync.dma_start(
                out=w_words[quad][:, g0 * 2 * D : (g0 + n) * 2 * D].bitcast(I32).rearrange("p (g n) -> p g n", g=n),
                in_=dram_words[first : first + n].rearrange("g p n -> p g n"),
            )

        def load_norm(tile, source):
            nc.sync.dma_start(out=tile, in_=source.rearrange("(p t) d -> p t d", t=TILES))

        def fetch(r):
            if r < n_rounds:
                tiles, first, n = rounds[r]
                raw = raw_pool.tile([P, len(tiles), n * K_PASS], BF16)
                together = TILES if n <= BANK_PASSES else 1
                m = min(n, QUAD)
                for j in range(0, len(tiles), together):
                    b, t = tiles[j]
                    for g in range(0, n, m):
                        nc.sync.dma_start(
                            out=raw[:, j : j + together, g * K_PASS : (g + m) * K_PASS],
                            in_=h_attn[b].rearrange("(p t) k -> p t k", t=TILES)[
                                :, t : t + together, (first + g) * K_PASS : (first + g + m) * K_PASS
                            ],
                        )
                raw_tiles[r] = raw
            if 1 <= r <= n_rounds and rounds[r - 1][1] not in fetched:
                fetched.add(rounds[r - 1][1])
                fetch_weights(rounds[r - 1][1], rounds[r - 1][2])
            if r == last_round[0] - 1:
                load_norm(bo_sb[:, 0], bo[0])
                load_norm(x_sb[:, 0], x[0])
            if r == n_rounds - 1:
                load_norm(bo_sb[:, 1], bo[1])
                load_norm(x_sb[:, 1], x[1])
            if r == n_rounds - 1:
                load_norm(gamma_sb[:], gamma)
                load_norm(beta_sb[:], beta)

        def scalar_share(r):
            return 2 if r == n_rounds - 1 else 0

        def sort_words(r):
            tiles, first, n = rounds[r]
            ordered = stage.tile([P, len(tiles), n, HALVES, P], F32)
            m = min(n, QUAD)
            for j in range(len(tiles)):
                view = raw_tiles[r][:, j, :].bitcast(F32).rearrange("r (g p u) -> r g u p", g=n, u=HALVES)
                for g in range(0, n, m):
                    mine = m - scalar_share(r) if (j, g + m) == (len(tiles) - 1, n) else m
                    nc.vector.tensor_copy(out=ordered[:, j, g : g + mine], in_=view[:, g : g + mine])
            ordered_tiles[r] = ordered

        def sort_rest(r):
            tiles, first, n = rounds[r]
            j = len(tiles) - 1
            g = n - scalar_share(r)
            if g < n:
                view = raw_tiles[r][:, j, :].bitcast(F32).rearrange("r (g p u) -> r g u p", g=n, u=HALVES)
                nc.scalar.copy(out=ordered_tiles[r][:, j, g:n], in_=view[:, g:n])

        def transpose(r):
            ordered = ordered_tiles[r]
            tiles, first, n = rounds[r]
            grouped = stage.tile([P, len(tiles) * n * P * PACK], BF16, align_bytes=64)
            grouped_words = grouped[:].bitcast(F32).rearrange(
                "p (j g r u) -> p j g r u", j=len(tiles), g=n, u=HALVES
            )
            for j in range(len(tiles)):
                for g0 in range(0, n, BANK_PASSES):
                    if (r, j) == (1, TILES - 1):
                        flipped = psum_acc.tile([P, BANK_PASSES, HALVES, P], F32, name="acc1%d" % (g0 // BANK_PASSES))
                    else:
                        flipped = psum_work.tile([P, BANK_PASSES, HALVES, P], F32, tag="work")
                    for g in range(BANK_PASSES):
                        for u in range(HALVES):
                            nc.tensor.transpose(flipped[:, g, u, :], ordered[:, j, g0 + g, u, :], identity[:])
                    nc.scalar.copy(
                        out=grouped_words[:, j, g0 : g0 + BANK_PASSES],
                        in_=flipped[:].rearrange("p g u r -> p g r u"),
                    )
            grouped_tiles[r] = grouped

        def quantise(r):
            grouped = grouped_tiles[r]
            tiles, first, n = rounds[r]
            codes = stage.tile([P, len(tiles) * n * P], U32, align_bytes=64)
            h_scales = stage.tile([P, len(tiles) * n * P], U8, align_bytes=64)
            step = min(n, QUAD) * P
            for first_col in range(0, len(tiles) * n * P, step):
                cols = slice(first_col, first_col + step)
                nc.vector.quantize_mx(
                    out=codes[:, cols].bitcast(FP8X4),
                    scales=h_scales[:, cols],
                    in_=grouped[:, first_col * PACK : (first_col + step) * PACK],
                )
            code_tiles[r] = (codes, h_scales)

        def multiply(r, passes=None):
            tiles, first, n = rounds[r]
            codes, h_scales = code_tiles[r]
            for j, (b, t) in enumerate(tiles):
                if first == 0:
                    acc[b][t] = psum_acc.tile([P, D], F32, name="acc%d%d" % (b, t))
                for g in passes or range(n):
                    quad, slot = divmod(first + g, QUAD)
                    tokens = slice((j * n + g) * P, (j * n + g + 1) * P)
                    nc.tensor.matmul_mx(
                        out=acc[b][t][:],
                        lhsT=codes[:, tokens].bitcast(FP8X4),
                        lhsT_scale=h_scales[:, tokens],
                        rhs=w_words[quad][:, slot * 2 * D : (slot + 1) * 2 * D].bitcast(FP4X4),
                        rhs_scale=w_scales[quad][:, slot * D : (slot + 1) * D],
                        start=(first + g == 0),
                        stop=(first + g == PASSES - 1),
                    )

        def add_bias_to_residual(b):
            extra = norm.tile([P, TILES * D], F32, name="extra%d" % b)
            nc.vector.tensor_tensor(
                out=extra[:],
                in0=bo_sb[:, b].rearrange("p t d -> p (t d)"),
                in1=x_sb[:, b].rearrange("p t d -> p (t d)"),
                op=ALU.add,
            )
            parts[b]["extra"] = extra

        def add_up(b, t, shift=None):
            o = norm.tile([P, D], F32, name="o%d%d" % (b, t))
            row_sum = norm.tile([P, 1], F32, name="row_sum%d%d" % (b, t))
            nc.vector.scalar_tensor_tensor(
                out=o[:],
                in0=acc[b][t][:],
                scalar=0.0 if shift is None else shift,
                in1=parts[b]["extra"][:, t * D : (t + 1) * D],
                op0=ALU.subtract,
                op1=ALU.add,
                accum_out=row_sum[:],
            )
            parts[b]["o", t] = o
            parts[b]["row_sum", t] = row_sum

        def sum_squares(b, t, bias):
            square = norm.tile([P, D], F32, name="square%d%d" % (b, t))
            square_sum = norm.tile([P, 1], F32, name="square_sum%d%d" % (b, t))
            nc.scalar.activation(
                out=square[:], in_=parts[b]["o", t][:], func=ACT.Square, bias=bias, scale=-1.0, accum_out=square_sum[:]
            )
            parts[b]["square_sum", t] = square_sum

        def average(bank, matrix, columns):
            result = psum_acc.tile([P, 1], F32, name=bank)
            for j, column in enumerate(columns):
                nc.tensor.matmul(
                    out=result[:], lhsT=matrix[:], rhs=column[:], start=(j == 0), stop=(j == len(columns) - 1)
                )
            return result

        def to_sbuf(name, value):
            copy = norm.tile([P, 1], F32, name=name)
            nc.vector.tensor_copy(out=copy[:], in_=value[:])
            return copy

        def scale_by_gamma(b, t, mean):
            centred = norm.tile([P, D], F32, name="centred%d%d" % (b, t))
            nc.vector.scalar_tensor_tensor(
                out=centred[:],
                in0=parts[b]["o", t][:],
                scalar=mean,
                in1=gamma_sb[:, t, :],
                op0=ALU.subtract,
                op1=ALU.mult,
            )
            parts[b]["centred", t] = centred

        def invert(b, variance, offset, sign=1.0):
            inv_std = norm.tile([P, 1], F32, name="inv_std%d" % b)
            nc.scalar.activation(
                out=inv_std[:], in_=variance[:], func=ACT.Abs_reciprocal_sqrt, bias=offset, scale=sign
            )
            parts[b]["inv_std"] = inv_std

        def normalise_and_store(b, t, pieces=1):
            result = norm.tile([P, D], F32, name="result%d%d" % (b, t))
            for j in range(pieces):
                cols = slice(j * D // pieces, (j + 1) * D // pieces)
                nc.vector.scalar_tensor_tensor(
                    out=result[:, cols],
                    in0=parts[b]["centred", t][:, cols],
                    scalar=parts[b]["inv_std"][:],
                    in1=beta_sb[:, t, cols],
                    op0=ALU.mult,
                    op1=ALU.add,
                )
                nc.sync.dma_start(
                    out=out[b].rearrange("(p t) d -> p t d", t=TILES)[:, t, cols], in_=result[:, cols]
                )

        for r in range(PREFETCH):
            fetch(r)
        for i in range(n_rounds + 1):
            if i - 2 >= 0:
                quantise(i - 2)
            if i < n_rounds:
                sort_words(i)
            if i == last_round[0] - 1:
                add_bias_to_residual(0)
            if i == n_rounds:
                add_bias_to_residual(1)
            if i - 1 >= 0:
                transpose(i - 1)
            if i < n_rounds:
                sort_rest(i)
                fetch(i + PREFETCH)
            if i - 2 >= 0 and i < n_rounds:
                multiply(i - 2)
        last = n_rounds - 1
        for t in range(TILES):
            add_up(0, t)
        multiply(last - 1)
        zero_mean = average("acc00", averager, (parts[0]["row_sum", 0], parts[0]["row_sum", 1]))
        quantise(last)
        multiply(last, range(6))
        mean = to_sbuf("mean0", zero_mean)
        for t in range(TILES):
            sum_squares(0, t, mean[:])
        add_up(1, 0)
        for t in range(TILES):
            scale_by_gamma(0, t, mean[:])
        shift_sum = average("acc10", tile_averager, (parts[1]["row_sum", 0],))
        multiply(last, range(6, 8))
        variance = average("acc01", averager, (parts[0]["square_sum", 0], parts[0]["square_sum", 1]))
        shift = to_sbuf("shift", shift_sum)
        sum_squares(1, 0, shift[:])
        invert(0, variance, eps[:])
        add_up(1, 1, shift[:])
        delta = average("acc00", averager, (parts[1]["row_sum", 1],))
        sum_squares(1, 1, zero[:])
        normalise_and_store(0, 0)
        mean = norm.tile([P, 1], F32, name="mean1")
        nc.vector.tensor_tensor(out=mean[:], in0=delta[:], in1=shift[:], op=ALU.add)
        scale_by_gamma(1, 1, delta[:])
        offset = norm.tile([P, 1], F32)
        nc.vector.scalar_tensor_tensor(
            out=offset[:], in0=delta[:], scalar=delta[:], in1=eps[:], op0=ALU.mult, op1=ALU.subtract
        )
        spread = average("acc11", averager, (parts[1]["square_sum", 0], parts[1]["square_sum", 1]))
        invert(1, spread, offset[:], -1.0)
        scale_by_gamma(1, 0, mean[:])
        normalise_and_store(0, 1)
        for t in range(TILES):
            normalise_and_store(1, t, 2)
